import numpy as np
import ml_dtypes


def mxq(x, axis, fmt="e4m3"):
    dtype, down = {"e4m3": (ml_dtypes.float8_e4m3fn, 7), "e5m2": (ml_dtypes.float8_e5m2, 14)}[fmt]
    v = np.moveaxis(np.asarray(x, np.float32).astype(ml_dtypes.bfloat16).astype(np.float64), axis, -1)
    blocks = v.reshape(v.shape[:-1] + (-1, 32))
    amax = np.abs(blocks).max(-1, keepdims=True)
    byte = np.maximum(np.where(amax > 0, np.frexp(amax)[1] - 1 + 127, 0) - down, 1)
    scale = np.exp2(byte - 127.0)
    codes = (blocks / scale).astype(np.float32).astype(dtype).astype(np.float64)
    return np.moveaxis((codes * scale).reshape(v.shape), -1, axis)


WIDE = False


def mx_kscale(k):
    if not WIDE:
        return np.ones(k)
    levels = np.array([10, -10, 5, -5, 0])
    if k % 512:
        return np.exp2(np.random.permutation(np.resize(levels, k // 32))).repeat(32)
    a = np.empty((k // 512, 16))
    for p in range(k // 512):
        a[p, :8] = np.random.permutation(np.resize(levels, 8))
        for g in range(8):
            far = levels[np.abs(levels - a[p, g]) >= 10]
            a[p, g + 8] = far[np.random.randint(len(far))]
    return np.exp2(a.ravel()).repeat(32)


BF16 = ml_dtypes.bfloat16


def bf(x):
    return np.asarray(x, np.float32).astype(BF16)


def f64(x):
    return np.asarray(x).astype(np.float64)


B, C, CI, N = 2, 1024, 512, 1024
EPS = 1e-5


def setup_inputs():
    s, t = mx_kscale(N), mx_kscale(CI)
    r = np.random.standard_normal
    return {"affinity": bf(r((B, N, N)) * 0.2 * s[None, None, :]),
            "g_x": bf(r((B, N, CI)) / s[None, :, None] * t[None, None, :]),
            "w_w": bf(r((C, CI)) * 1.5 / (0.2 * np.sqrt(N) * np.sqrt(CI)) / t[None, :]),
            "w_b": bf(r(C) * 0.3),
            "bn_gamma": bf(r(C)),
            "bn_beta": bf(r(C) * 0.5),
            "bn_mean": bf(r(C) * 0.5),
            "bn_var": bf(np.random.uniform(0.5, 1.5, C)),
            "x": bf(r((B, C, N)))}


def reference(affinity, g_x, w_w, w_b, bn_gamma, bn_beta, bn_mean, bn_var, x):
    y = (mxq(f64(affinity), 2, "e4m3") @ mxq(f64(g_x), 1, "e4m3")).transpose(0, 2, 1)
    wy = (mxq(f64(w_w), 1, "e4m3") @ mxq(y, 1, "e4m3")) + f64(w_b)[None, :, None]
    inv_std = 1.0 / np.sqrt(f64(bn_var) + EPS)
    wy = f64(bn_gamma)[None, :, None] * (wy - f64(bn_mean)[None, :, None]) * inv_std[None, :, None] + f64(bn_beta)[None, :, None]
    return wy + f64(x)

@@ -1,0 +1,303 @@
+from contextlib import ExitStack
+
+import concourse.masks as masks
+import concourse.mybir as mybir
+
+F32 = mybir.dt.float32
+BF16 = mybir.dt.bfloat16
+U32 = mybir.dt.uint32
+U8 = mybir.dt.uint8
+FP8X4 = mybir.dt.float8_e4m3fn_x4
+ALU = mybir.AluOpType
+ACT = mybir.ActivationFunctionType
+
+P = 128
+PACK = 4
+K_PASS = P * PACK
+
+BATCH = 2
+POINTS = 1024
+INNER = 512
+CHANNELS = 1024
+EPS = 1e-5
+
+SOURCE_PASSES = POINTS // K_PASS
+INNER_TILES = INNER // P
+CHANNEL_TILES = CHANNELS // P
+CHUNK = 2 * P
+CHUNKS = POINTS // CHUNK
+HALF = 512
+HALVES = POINTS // HALF
+
+FLOPS = 2 * BATCH * POINTS * POINTS * INNER + 2 * BATCH * CHANNELS * INNER * POINTS
+
+
+def tile_sgcam_pb_kernel(
+    tc, affinity, g_x, w_w, w_b, bn_gamma, bn_beta, bn_mean, bn_var, x, out
+):
+    nc = tc.nc
+    with ExitStack() as ctx:
+        const = ctx.enter_context(tc.tile_pool(name="const", bufs=1))
+        loads = ctx.enter_context(tc.tile_pool(name="loads", bufs=1))
+        keep = ctx.enter_context(tc.tile_pool(name="keep", bufs=1))
+        stage = ctx.enter_context(tc.tile_pool(name="stage", bufs=2))
+        chunk_pool = ctx.enter_context(tc.tile_pool(name="chunk", bufs=4))
+        banks = ctx.enter_context(tc.psum_pool(name="banks", bufs=8))
+        ctx.enter_context(tc.manual_schedule())
+
+        def load_values(b, g):
+            raw = loads.tile([P, PACK, INNER], BF16, name="gx_raw%d%d" % (b, g))
+            nc.sync.dma_start(
+                out=raw[:], in_=g_x[b, g * K_PASS : (g + 1) * K_PASS, :].rearrange("(q j) c -> q j c", j=PACK)
+            )
+            return raw
+
+        def load_affinity(b, i):
+            rows = loads.tile([P, 2, POINTS], BF16, name="aff%d%d" % (b, i))
+            nc.sync.dma_start(
+                out=rows[:],
+                in_=affinity[b, i * CHUNK : (i + 1) * CHUNK, :].rearrange("(p j) m -> p j m", j=2),
+            )
+            return rows
+
+        def load_residual(b, h):
+            rows = loads.tile([P, CHANNEL_TILES // 2, POINTS], BF16, name="x%d%d" % (b, h))
+            half_rows = slice(h * CHANNEL_TILES // 2, (h + 1) * CHANNEL_TILES // 2)
+            nc.sync.dma_start(out=rows[:], in_=x[b].rearrange("(p r) n -> p r n", r=CHANNEL_TILES)[:, half_rows, :])
+            return rows
+
+        def load_vector(vec, name):
+            rows = const.tile([P, CHANNEL_TILES], BF16, name=name)
+            nc.scalar.dma_start(out=rows[:], in_=vec.rearrange("(p r) -> p r", r=CHANNEL_TILES))
+            return rows
+
+        var_bf = load_vector(bn_var, "var_bf")
+        gamma_bf = load_vector(bn_gamma, "gamma_bf")
+        bias_bf = load_vector(w_b, "bias_bf")
+        mean_bf = load_vector(bn_mean, "mean_bf")
+        beta_bf = load_vector(bn_beta, "beta_bf")
+
+        gx_raw = {}
+        aff = {}
+        x_rows = {}
+        for g in range(SOURCE_PASSES):
+            gx_raw[0, g] = load_values(0, g)
+        for i in range(CHUNKS):
+            aff[0, i] = load_affinity(0, i)
+        w_rows = loads.tile([P, CHANNEL_TILES, INNER], BF16)
+        nc.sync.dma_start(out=w_rows[:], in_=w_w.rearrange("(p r) k -> p r k", r=CHANNEL_TILES))
+        for h in range(2):
+            x_rows[0, h] = load_residual(0, h)
+        for g in range(SOURCE_PASSES):
+            gx_raw[1, g] = load_values(1, g)
+        for i in range(CHUNKS):
+            aff[1, i] = load_affinity(1, i)
+        for h in range(2):
+            x_rows[1, h] = load_residual(1, h)
+
+        ident_f32 = const.tile([P, P], F32)
+        masks.make_identity(nc, ident_f32[:])
+
+        gx_grouped = {}
+        gx_codes = {}
+        gx_scales = {}
+
+        def regroup_values(b, g):
+            grouped = stage.tile([P, INNER, PACK], BF16, name="gx_grouped", align_bytes=64)
+            regroup = nc.vector.tensor_copy if g == 0 else nc.scalar.copy
+            regroup(
+                out=grouped[:].rearrange("q (t m) j -> q t m j", t=INNER_TILES),
+                in_=gx_raw[b, g][:].rearrange("q j (m t) -> q t m j", t=INNER_TILES),
+            )
+            gx_grouped[b, g] = grouped
+
+        def quantise_values(b, g):
+            codes = keep.tile([P, INNER], U32, name="gx_codes%d%d" % (b, g), align_bytes=64)
+            scales = keep.tile([P, INNER], U8, name="gx_scales%d%d" % (b, g), align_bytes=64)
+            nc.vector.quantize_mx(
+                out=codes[:].bitcast(FP8X4), scales=scales[:], in_=gx_grouped[b, g][:].rearrange("q c t -> q (c t)")
+            )
+            gx_codes[b, g] = codes
+            gx_scales[b, g] = scales
+
+        aff_grouped = {}
+        aff_codes = {}
+        aff_scales = {}
+
+        def flip_affinity(b, i):
+            words = aff[b, i][:].rearrange("p j m -> p (j m)").bitcast(F32)
+            grouped = chunk_pool.tile([P, SOURCE_PASSES * CHUNK * PACK], BF16, name="aff_grouped", align_bytes=64)
+            grouped_words = grouped[:].bitcast(F32).rearrange(
+                "q (g p j u) -> q g p j u", g=SOURCE_PASSES, j=2, u=2
+            )
+            for g in range(SOURCE_PASSES):
+                flipped = banks.tile([P, 2, 2, P], F32, name="flipped", tag="bank")
+                for j in range(2):
+                    for u in range(2):
+                        first = j * (POINTS // 2) + g * (K_PASS // 2) + u
+                        nc.tensor.transpose(flipped[:, j, u, :], words[:, first : first + 2 * P - 1 : 2], ident_f32[:])
+                nc.scalar.copy(out=grouped_words[:, g], in_=flipped[:].rearrange("q j u p -> q p j u"))
+            aff_grouped[b, i] = grouped
+
+        def quantise_affinity(b, i):
+            codes = chunk_pool.tile([P, SOURCE_PASSES * CHUNK], U32, name="aff_codes", align_bytes=64)
+            scales = chunk_pool.tile([P, SOURCE_PASSES * CHUNK], U8, name="aff_scales", align_bytes=64)
+            nc.vector.quantize_mx(out=codes[:].bitcast(FP8X4), scales=scales[:], in_=aff_grouped[b, i][:])
+            aff_codes[b, i] = codes
+            aff_scales[b, i] = scales
+
+        y_grouped = {}
+        y_codes = {}
+        y_scales = {}
+
+        def aggregate(b, i):
+            h, k = divmod(i, HALF // CHUNK)
+            if k == 0:
+                y_grouped[b, h] = stage.tile([P, HALF, PACK], BF16, name="y_grouped", align_bytes=64)
+            for s in range(CHUNK // P):
+                y_bank = banks.tile([P, INNER_TILES, P], F32, name="y_bank", tag="bank")
+                for t in range(INNER_TILES):
+                    for g in range(SOURCE_PASSES):
+                        ci = slice(t * P, (t + 1) * P)
+                        pts = slice(g * CHUNK + s * P, g * CHUNK + (s + 1) * P)
+                        nc.tensor.matmul_mx(
+                            out=y_bank[:, t, :],
+                            lhsT=gx_codes[b, g][:, ci].bitcast(FP8X4),
+                            lhsT_scale=gx_scales[b, g][:, ci],
+                            rhs=aff_codes[b, i][:, pts].bitcast(FP8X4),
+                            rhs_scale=aff_scales[b, i][:, pts],
+                            start=(g == 0),
+                            stop=(g == SOURCE_PASSES - 1),
+                        )
+                lo = k * CHUNK + s * P
+                nc.scalar.copy(out=y_grouped[b, h][:, lo : lo + P, :], in_=y_bank[:].rearrange("q t n -> q n t"))
+
+        def quantise_y(b, h):
+            codes = keep.tile([P, HALF], U32, name="y_codes%d%d" % (b, h), align_bytes=64)
+            scales = keep.tile([P, HALF], U8, name="y_scales%d%d" % (b, h), align_bytes=64)
+            nc.vector.quantize_mx(
+                out=codes[:].bitcast(FP8X4), scales=scales[:], in_=y_grouped[b, h][:].rearrange("q n t -> q (n t)")
+            )
+            y_codes[b, h] = codes
+            y_scales[b, h] = scales
+
+        w_grouped = keep.tile([P, CHANNEL_TILES, P, PACK], BF16, align_bytes=64)
+        w_codes = keep.tile([P, CHANNELS], U32, align_bytes=64)
+        w_scales = keep.tile([P, CHANNELS], U8, align_bytes=64)
+
+        def flip_weights(pair):
+            words = w_rows[:].rearrange("p r k -> p (r k)").bitcast(F32)
+            flipped = banks.tile([P, 2, 2, P], F32, name="w_flipped", tag="bank")
+            for k in range(2):
+                for u in range(2):
+                    first = (2 * pair + k) * (INNER // 2) + u
+                    nc.tensor.transpose(flipped[:, k, u, :], words[:, first : first + 2 * P - 1 : 2], ident_f32[:])
+            copy_out = nc.scalar.copy if pair % 2 == 0 else nc.vector.tensor_copy
+            grouped_words = w_grouped[:].rearrange("q r p t -> q (r p t)").bitcast(F32)
+            copy_out(
+                out=grouped_words[:, 2 * pair * 2 * P : (2 * pair + 2) * 2 * P].rearrange("q (k p u) -> q k p u", k=2, u=2),
+                in_=flipped[:].rearrange("q k u p -> q k p u"),
+            )
+
+        def quantise_weights():
+            nc.vector.quantize_mx(
+                out=w_codes[:].bitcast(FP8X4), scales=w_scales[:], in_=w_grouped[:].rearrange("q r p t -> q (r p t)")
+            )
+
+        std = const.tile([P, CHANNEL_TILES], F32)
+        gain = const.tile([P, CHANNEL_TILES], F32)
+        shift = const.tile([P, CHANNEL_TILES], F32)
+
+        def start_batch_norm():
+            nc.vector.tensor_scalar_add(out=std[:], in0=var_bf[:], scalar1=EPS)
+            nc.scalar.sqrt(out=std[:], in_=std[:])
+
+        def finish_batch_norm():
+            nc.vector.reciprocal(out=gain[:], in_=std[:])
+            nc.vector.tensor_mul(out=gain[:], in0=gain[:], in1=gamma_bf[:])
+            nc.vector.tensor_sub(out=shift[:], in0=bias_bf[:], in1=mean_bf[:])
+            nc.vector.tensor_mul(out=shift[:], in0=shift[:], in1=gain[:])
+            nc.vector.tensor_add(out=shift[:], in0=shift[:], in1=beta_bf[:])
+
+        results = {}
+
+        def shift_residual(b, r, on_gpsimd=False):
+            result = keep.tile([P, POINTS], F32, name="result%d%d" % (b, r))
+            x_tile = x_rows[b, r // (CHANNEL_TILES // 2)][:, r % (CHANNEL_TILES // 2), :]
+            if on_gpsimd:
+                nc.gpsimd.tensor_scalar(
+                    out=result[:], in0=x_tile, scalar1=1.0, scalar2=shift[:, r : r + 1], op0=ALU.mult, op1=ALU.add
+                )
+            else:
+                nc.scalar.activation(out=result[:], in_=x_tile, func=ACT.Identity, bias=shift[:, r : r + 1])
+            results[b, r] = result
+
+        def project(b, r):
+            chans = slice(r * P, (r + 1) * P)
+            result = results[b, r]
+            out_tile = out[b].rearrange("(p r) n -> p r n", r=CHANNEL_TILES)[:, r, :]
+            last_tile = b == BATCH - 1 and r == CHANNEL_TILES - 1
+            for h in range(HALVES):
+                acc = banks.tile([P, HALF], F32, name="acc", tag="bank")
+                nc.tensor.matmul_mx(
+                    out=acc[:],
+                    lhsT=w_codes[:, chans].bitcast(FP8X4),
+                    lhsT_scale=w_scales[:, chans],
+                    rhs=y_codes[b, h][:].bitcast(FP8X4),
+                    rhs_scale=y_scales[b, h][:],
+                    start=True,
+                    stop=True,
+                )
+                pts = slice(h * HALF, (h + 1) * HALF)
+                nc.vector.scalar_tensor_tensor(
+                    out=result[:, pts],
+                    in0=acc[:],
+                    scalar=gain[:, r : r + 1],
+                    in1=result[:, pts],
+                    op0=ALU.mult,
+                    op1=ALU.add,
+                )
+                if last_tile:
+                    nc.sync.dma_start(out=out_tile[:, pts], in_=result[:, pts])
+            if not last_tile:
+                nc.sync.dma_start(out=out_tile, in_=result[:])
+
+        AHEAD = 2
+        start_batch_norm()
+        for b in range(BATCH):
+            for g in range(SOURCE_PASSES):
+                regroup_values(b, g)
+            if b == 0:
+                finish_batch_norm()
+            else:
+                quantise_y(b - 1, HALVES - 1)
+            for g in range(SOURCE_PASSES):
+                quantise_values(b, g)
+            for i in range(AHEAD):
+                flip_affinity(b, i)
+            for i in range(CHUNKS):
+                quantise_affinity(b, i)
+                if b > 0:
+                    project(b - 1, 2 * i)
+                    project(b - 1, 2 * i + 1)
+                if i + AHEAD < CHUNKS:
+                    flip_affinity(b, i + AHEAD)
+                elif b == 0:
+                    flip_weights(2 * (i + AHEAD - CHUNKS))
+                    flip_weights(2 * (i + AHEAD - CHUNKS) + 1)
+                aggregate(b, i)
+                if i == CHUNKS - 2:
+                    quantise_y(b, 0)
+                if b > 0 and i < CHUNKS // 2:
+                    shift_residual(b - 1, CHANNEL_TILES // 2 + 2 * i)
+                    shift_residual(b - 1, CHANNEL_TILES // 2 + 2 * i + 1)
+            if b < BATCH - 1:
+                for r in range(CHANNEL_TILES // 2):
+                    shift_residual(b, r, on_gpsimd=True)
+                quantise_weights()
+            else:
+                for r in range(CHANNEL_TILES):
+                    shift_residual(b, r)
+        quantise_y(BATCH - 1, HALVES - 1)
+        for r in range(CHANNEL_TILES):
+            project(BATCH - 1, r)

@@ -28,6 +28,8 @@ CHUNK = 2 * P
 CHUNKS = POINTS // CHUNK
 HALF = 512
 HALVES = POINTS // HALF
+STEPS = BATCH * CHUNKS
+AHEAD = 2
 
 FLOPS = 2 * BATCH * POINTS * POINTS * INNER + 2 * BATCH * CHANNELS * INNER * POINTS
 
@@ -68,32 +70,35 @@ def tile_sgcam_pb_kernel(
 
         def load_vector(vec, name):
             rows = const.tile([P, CHANNEL_TILES], BF16, name=name)
-            nc.scalar.dma_start(out=rows[:], in_=vec.rearrange("(p r) -> p r", r=CHANNEL_TILES))
+            nc.sync.dma_start(out=rows[:], in_=vec.rearrange("(p r) -> p r", r=CHANNEL_TILES))
             return rows
 
+        gx_raw = {}
+        aff = {}
+        x_rows = {}
+        aff[0, 0] = load_affinity(0, 0)
+        gx_raw[0, 0] = load_values(0, 0)
+        gx_raw[0, 1] = load_values(0, 1)
+        aff[0, 1] = load_affinity(0, 1)
+        aff[0, 2] = load_affinity(0, 2)
+        aff[0, 3] = load_affinity(0, 3)
+        w_rows = loads.tile([P, CHANNEL_TILES, INNER], BF16)
+        nc.sync.dma_start(out=w_rows[:], in_=w_w.rearrange("(p r) k -> p r k", r=CHANNEL_TILES))
+        aff[1, 0] = load_affinity(1, 0)
         var_bf = load_vector(bn_var, "var_bf")
         gamma_bf = load_vector(bn_gamma, "gamma_bf")
         bias_bf = load_vector(w_b, "bias_bf")
         mean_bf = load_vector(bn_mean, "mean_bf")
         beta_bf = load_vector(bn_beta, "beta_bf")
-
-        gx_raw = {}
-        aff = {}
-        x_rows = {}
-        for g in range(SOURCE_PASSES):
-            gx_raw[0, g] = load_values(0, g)
-        for i in range(CHUNKS):
-            aff[0, i] = load_affinity(0, i)
-        w_rows = loads.tile([P, CHANNEL_TILES, INNER], BF16)
-        nc.sync.dma_start(out=w_rows[:], in_=w_w.rearrange("(p r) k -> p r k", r=CHANNEL_TILES))
-        for h in range(2):
-            x_rows[0, h] = load_residual(0, h)
-        for g in range(SOURCE_PASSES):
-            gx_raw[1, g] = load_values(1, g)
-        for i in range(CHUNKS):
-            aff[1, i] = load_affinity(1, i)
-        for h in range(2):
-            x_rows[1, h] = load_residual(1, h)
+        gx_raw[1, 0] = load_values(1, 0)
+        gx_raw[1, 1] = load_values(1, 1)
+        aff[1, 1] = load_affinity(1, 1)
+        x_rows[0, 0] = load_residual(0, 0)
+        aff[1, 2] = load_affinity(1, 2)
+        aff[1, 3] = load_affinity(1, 3)
+        x_rows[0, 1] = load_residual(0, 1)
+        x_rows[1, 0] = load_residual(1, 0)
+        x_rows[1, 1] = load_residual(1, 1)
 
         ident_f32 = const.tile([P, P], F32)
         masks.make_identity(nc, ident_f32[:])
@@ -102,13 +107,15 @@ def tile_sgcam_pb_kernel(
         gx_codes = {}
         gx_scales = {}
 
-        def regroup_values(b, g):
+        def regroup_values(b, g, shared=False):
             grouped = stage.tile([P, INNER, PACK], BF16, name="gx_grouped", align_bytes=64)
-            regroup = nc.vector.tensor_copy if g == 0 else nc.scalar.copy
-            regroup(
-                out=grouped[:].rearrange("q (t m) j -> q t m j", t=INNER_TILES),
-                in_=gx_raw[b, g][:].rearrange("q j (m t) -> q t m j", t=INNER_TILES),
-            )
+            split = P if not shared else 3 * P // 4
+            for regroup, lo, hi in ((nc.vector.tensor_copy, 0, split), (nc.scalar.copy, split, P)):
+                if lo < hi:
+                    regroup(
+                        out=grouped[:].rearrange("q (t m) j -> q t m j", t=INNER_TILES)[:, :, lo:hi],
+                        in_=gx_raw[b, g][:].rearrange("q j (m t) -> q t m j", t=INNER_TILES)[:, :, lo:hi],
+                    )
             gx_grouped[b, g] = grouped
 
         def quantise_values(b, g):
@@ -192,7 +199,7 @@ def tile_sgcam_pb_kernel(
                 for u in range(2):
                     first = (2 * pair + k) * (INNER // 2) + u
                     nc.tensor.transpose(flipped[:, k, u, :], words[:, first : first + 2 * P - 1 : 2], ident_f32[:])
-            copy_out = nc.scalar.copy if pair % 2 == 0 else nc.vector.tensor_copy
+            copy_out = nc.scalar.copy
             grouped_words = w_grouped[:].rearrange("q r p t -> q (r p t)").bitcast(F32)
             copy_out(
                 out=grouped_words[:, 2 * pair * 2 * P : (2 * pair + 2) * 2 * P].rearrange("q (k p u) -> q k p u", k=2, u=2),
@@ -209,25 +216,34 @@ def tile_sgcam_pb_kernel(
         shift = const.tile([P, CHANNEL_TILES], F32)
 
         def start_batch_norm():
-            nc.vector.tensor_scalar_add(out=std[:], in0=var_bf[:], scalar1=EPS)
+            warm = const.tile([P, 1], F32)
+            nc.vector.memset(warm[:], 1.0)
+            nc.scalar.sqrt(out=warm[:], in_=warm[:])
+
+        def batch_norm_std():
+            nc.gpsimd.tensor_scalar(
+                out=std[:], in0=var_bf[:], scalar1=1.0, scalar2=EPS, op0=ALU.mult, op1=ALU.add
+            )
+            nc.gpsimd.tensor_sub(out=shift[:], in0=bias_bf[:], in1=mean_bf[:])
             nc.scalar.sqrt(out=std[:], in_=std[:])
 
         def finish_batch_norm():
             nc.vector.reciprocal(out=gain[:], in_=std[:])
-            nc.vector.tensor_mul(out=gain[:], in0=gain[:], in1=gamma_bf[:])
-            nc.vector.tensor_sub(out=shift[:], in0=bias_bf[:], in1=mean_bf[:])
-            nc.vector.tensor_mul(out=shift[:], in0=shift[:], in1=gain[:])
-            nc.vector.tensor_add(out=shift[:], in0=shift[:], in1=beta_bf[:])
+            nc.gpsimd.tensor_mul(out=gain[:], in0=gain[:], in1=gamma_bf[:])
+            nc.gpsimd.tensor_mul(out=shift[:], in0=shift[:], in1=gain[:])
+            nc.gpsimd.tensor_add(out=shift[:], in0=shift[:], in1=beta_bf[:])
 
         results = {}
 
-        def shift_residual(b, r, on_gpsimd=False):
+        def shift_residual(b, r, engine):
             result = keep.tile([P, POINTS], F32, name="result%d%d" % (b, r))
             x_tile = x_rows[b, r // (CHANNEL_TILES // 2)][:, r % (CHANNEL_TILES // 2), :]
-            if on_gpsimd:
+            if engine == 'G':
                 nc.gpsimd.tensor_scalar(
                     out=result[:], in0=x_tile, scalar1=1.0, scalar2=shift[:, r : r + 1], op0=ALU.mult, op1=ALU.add
                 )
+            elif engine == 'V':
+                nc.vector.tensor_scalar_add(out=result[:], in0=x_tile, scalar1=shift[:, r : r + 1])
             else:
                 nc.scalar.activation(out=result[:], in_=x_tile, func=ACT.Identity, bias=shift[:, r : r + 1])
             results[b, r] = result
@@ -262,42 +278,44 @@ def tile_sgcam_pb_kernel(
             if not last_tile:
                 nc.sync.dma_start(out=out_tile, in_=result[:])
 
-        AHEAD = 2
         start_batch_norm()
-        for b in range(BATCH):
-            for g in range(SOURCE_PASSES):
-                regroup_values(b, g)
-            if b == 0:
+        for g in range(SOURCE_PASSES):
+            regroup_values(0, g, shared=True)
+        flip_affinity(0, 0)
+        for g in range(SOURCE_PASSES):
+            quantise_values(0, g)
+        quantise_affinity(0, 0)
+        flip_affinity(0, 1)
+        for c in range(STEPS):
+            if c + AHEAD < STEPS:
+                flip_affinity(*divmod(c + AHEAD, CHUNKS))
+            aggregate(*divmod(c, CHUNKS))
+            if c == 1:
+                batch_norm_std()
+            if c + 1 < STEPS:
+                quantise_affinity(*divmod(c + 1, CHUNKS))
+            if c == 2:
                 finish_batch_norm()
-            else:
-                quantise_y(b - 1, HALVES - 1)
-            for g in range(SOURCE_PASSES):
-                quantise_values(b, g)
-            for i in range(AHEAD):
-                flip_affinity(b, i)
-            for i in range(CHUNKS):
-                quantise_affinity(b, i)
-                if b > 0:
-                    project(b - 1, 2 * i)
-                    project(b - 1, 2 * i + 1)
-                if i + AHEAD < CHUNKS:
-                    flip_affinity(b, i + AHEAD)
-                elif b == 0:
-                    flip_weights(2 * (i + AHEAD - CHUNKS))
-                    flip_weights(2 * (i + AHEAD - CHUNKS) + 1)
-                aggregate(b, i)
-                if i == CHUNKS - 2:
-                    quantise_y(b, 0)
-                if b > 0 and i < CHUNKS // 2:
-                    shift_residual(b - 1, CHANNEL_TILES // 2 + 2 * i)
-                    shift_residual(b - 1, CHANNEL_TILES // 2 + 2 * i + 1)
-            if b < BATCH - 1:
-                for r in range(CHANNEL_TILES // 2):
-                    shift_residual(b, r, on_gpsimd=True)
+            if c % 2 == 0 and c > 0:
+                quantise_y(*divmod(c // 2 - 1, HALVES))
+            if c == STEPS - 1:
+                quantise_y(BATCH - 1, HALVES - 1)
+            if CHUNKS - 1 <= c < STEPS - 1:
+                shift_residual(0, 2 * (c - CHUNKS + 1), "V")
+                shift_residual(0, 2 * (c - CHUNKS + 1) + 1, "S")
+            if c in (1, 2):
+                flip_weights(2 * (c - 1))
+                flip_weights(2 * (c - 1) + 1)
+            if c == 2:
+                for g in range(SOURCE_PASSES):
+                    regroup_values(1, g)
+                for g in range(SOURCE_PASSES):
+                    quantise_values(1, g)
+            if c == 3:
                 quantise_weights()
-            else:
-                for r in range(CHANNEL_TILES):
-                    shift_residual(b, r)
-        quantise_y(BATCH - 1, HALVES - 1)
+            if c >= CHUNKS:
+                project(0, 2 * (c - CHUNKS))
+                project(0, 2 * (c - CHUNKS) + 1)
         for r in range(CHANNEL_TILES):
-            project(BATCH - 1, r)
+            shift_residual(1, r, "S")
+            project(1, r)

@@ -103,6 +103,14 @@ def tile_sgcam_pb_kernel(
         ident_f32 = const.tile([P, P], F32)
         masks.make_identity(nc, ident_f32[:])
 
+        dummy = const.tile([P, HALF], BF16)
+        nc.vector.memset(dummy[:], 0.0)
+
+        def keep_warm(count):
+            bank = banks.tile([P, HALF], F32, name="warm_bank", tag="bank")
+            for k in range(count):
+                nc.tensor.matmul(out=bank[:], lhsT=dummy[:, :P], rhs=dummy[:], start=True, stop=True)
+
         gx_grouped = {}
         gx_codes = {}
         gx_scales = {}
@@ -281,14 +289,19 @@ def tile_sgcam_pb_kernel(
         start_batch_norm()
         for g in range(SOURCE_PASSES):
             regroup_values(0, g, shared=True)
+        keep_warm(4)
         flip_affinity(0, 0)
+        keep_warm(4)
         for g in range(SOURCE_PASSES):
             quantise_values(0, g)
         quantise_affinity(0, 0)
         flip_affinity(0, 1)
+        keep_warm(2)
         for c in range(STEPS):
             if c + AHEAD < STEPS:
                 flip_affinity(*divmod(c + AHEAD, CHUNKS))
+            if c == 0:
+                keep_warm(2)
             aggregate(*divmod(c, CHUNKS))
             if c == 1:
                 batch_norm_std()

@@ -68,6 +68,12 @@ def tile_sgcam_pb_kernel(
             nc.sync.dma_start(out=rows[:], in_=x[b].rearrange("(p r) n -> p r n", r=CHANNEL_TILES)[:, half_rows, :])
             return rows
 
+        def load_weights(h):
+            rows = loads.tile([P, CHANNEL_TILES // 2, INNER], BF16, name="w%d" % h)
+            half_rows = slice(h * CHANNEL_TILES // 2, (h + 1) * CHANNEL_TILES // 2)
+            nc.sync.dma_start(out=rows[:], in_=w_w.rearrange("(p r) k -> p r k", r=CHANNEL_TILES)[:, half_rows, :])
+            return rows
+
         def load_vector(vec, name):
             rows = const.tile([P, CHANNEL_TILES], BF16, name=name)
             nc.sync.dma_start(out=rows[:], in_=vec.rearrange("(p r) -> p r", r=CHANNEL_TILES))
@@ -75,23 +81,24 @@ def tile_sgcam_pb_kernel(
 
         gx_raw = {}
         aff = {}
+        w_rows = {}
         x_rows = {}
-        aff[0, 0] = load_affinity(0, 0)
         gx_raw[0, 0] = load_values(0, 0)
+        aff[0, 0] = load_affinity(0, 0)
         gx_raw[0, 1] = load_values(0, 1)
         aff[0, 1] = load_affinity(0, 1)
         aff[0, 2] = load_affinity(0, 2)
         aff[0, 3] = load_affinity(0, 3)
-        w_rows = loads.tile([P, CHANNEL_TILES, INNER], BF16)
-        nc.sync.dma_start(out=w_rows[:], in_=w_w.rearrange("(p r) k -> p r k", r=CHANNEL_TILES))
+        w_rows[0] = load_weights(0)
+        w_rows[1] = load_weights(1)
+        gx_raw[1, 0] = load_values(1, 0)
+        gx_raw[1, 1] = load_values(1, 1)
         aff[1, 0] = load_affinity(1, 0)
         var_bf = load_vector(bn_var, "var_bf")
         gamma_bf = load_vector(bn_gamma, "gamma_bf")
         bias_bf = load_vector(w_b, "bias_bf")
         mean_bf = load_vector(bn_mean, "mean_bf")
         beta_bf = load_vector(bn_beta, "beta_bf")
-        gx_raw[1, 0] = load_values(1, 0)
-        gx_raw[1, 1] = load_values(1, 1)
         aff[1, 1] = load_affinity(1, 1)
         x_rows[0, 0] = load_residual(0, 0)
         aff[1, 2] = load_affinity(1, 2)
@@ -165,11 +172,11 @@ def tile_sgcam_pb_kernel(
         y_codes = {}
         y_scales = {}
 
-        def aggregate(b, i):
+        def aggregate(b, i, blocks=range(CHUNK // P)):
             h, k = divmod(i, HALF // CHUNK)
-            if k == 0:
+            if k == 0 and 0 in blocks:
                 y_grouped[b, h] = stage.tile([P, HALF, PACK], BF16, name="y_grouped", align_bytes=64)
-            for s in range(CHUNK // P):
+            for s in blocks:
                 y_bank = banks.tile([P, INNER_TILES, P], F32, name="y_bank", tag="bank")
                 for t in range(INNER_TILES):
                     for g in range(SOURCE_PASSES):
@@ -200,14 +207,13 @@ def tile_sgcam_pb_kernel(
         w_codes = keep.tile([P, CHANNELS], U32, align_bytes=64)
         w_scales = keep.tile([P, CHANNELS], U8, align_bytes=64)
 
-        def flip_weights(pair):
-            words = w_rows[:].rearrange("p r k -> p (r k)").bitcast(F32)
+        def flip_weights(pair, copy_out=nc.scalar.copy):
+            words = w_rows[pair // 2][:].rearrange("p r k -> p (r k)").bitcast(F32)
             flipped = banks.tile([P, 2, 2, P], F32, name="w_flipped", tag="bank")
             for k in range(2):
                 for u in range(2):
-                    first = (2 * pair + k) * (INNER // 2) + u
+                    first = (2 * (pair % 2) + k) * (INNER // 2) + u
                     nc.tensor.transpose(flipped[:, k, u, :], words[:, first : first + 2 * P - 1 : 2], ident_f32[:])
-            copy_out = nc.scalar.copy
             grouped_words = w_grouped[:].rearrange("q r p t -> q (r p t)").bitcast(F32)
             copy_out(
                 out=grouped_words[:, 2 * pair * 2 * P : (2 * pair + 2) * 2 * P].rearrange("q (k p u) -> q k p u", k=2, u=2),
@@ -223,21 +229,17 @@ def tile_sgcam_pb_kernel(
         gain = const.tile([P, CHANNEL_TILES], F32)
         shift = const.tile([P, CHANNEL_TILES], F32)
 
-        def start_batch_norm():
-            warm = const.tile([P, 1], F32)
-            nc.vector.memset(warm[:], 1.0)
-            nc.scalar.sqrt(out=warm[:], in_=warm[:])
+        def load_function_table():
+            nc.scalar.activation(out=shift[:, :1], in_=dummy[:, :1], func=ACT.Identity)
 
-        def batch_norm_std():
+        def fold_batch_norm():
             nc.gpsimd.tensor_scalar(
                 out=std[:], in0=var_bf[:], scalar1=1.0, scalar2=EPS, op0=ALU.mult, op1=ALU.add
             )
+            nc.gpsimd.memset(gain[:], -0.5)
+            nc.gpsimd.tensor_tensor(out=std[:], in0=std[:], in1=gain[:], op=ALU.pow)
+            nc.gpsimd.tensor_mul(out=gain[:], in0=std[:], in1=gamma_bf[:])
             nc.gpsimd.tensor_sub(out=shift[:], in0=bias_bf[:], in1=mean_bf[:])
-            nc.scalar.sqrt(out=std[:], in_=std[:])
-
-        def finish_batch_norm():
-            nc.vector.reciprocal(out=gain[:], in_=std[:])
-            nc.gpsimd.tensor_mul(out=gain[:], in0=gain[:], in1=gamma_bf[:])
             nc.gpsimd.tensor_mul(out=shift[:], in0=shift[:], in1=gain[:])
             nc.gpsimd.tensor_add(out=shift[:], in0=shift[:], in1=beta_bf[:])
 
@@ -256,12 +258,12 @@ def tile_sgcam_pb_kernel(
                 nc.scalar.activation(out=result[:], in_=x_tile, func=ACT.Identity, bias=shift[:, r : r + 1])
             results[b, r] = result
 
-        def project(b, r):
+        def project(b, r, halves=range(HALVES)):
             chans = slice(r * P, (r + 1) * P)
             result = results[b, r]
             out_tile = out[b].rearrange("(p r) n -> p r n", r=CHANNEL_TILES)[:, r, :]
             last_tile = b == BATCH - 1 and r == CHANNEL_TILES - 1
-            for h in range(HALVES):
+            for h in halves:
                 acc = banks.tile([P, HALF], F32, name="acc", tag="bank")
                 nc.tensor.matmul_mx(
                     out=acc[:],
@@ -283,51 +285,57 @@ def tile_sgcam_pb_kernel(
                 )
                 if last_tile:
                     nc.sync.dma_start(out=out_tile[:, pts], in_=result[:, pts])
-            if not last_tile:
-                nc.sync.dma_start(out=out_tile, in_=result[:])
+                elif h == HALVES - 1:
+                    nc.sync.dma_start(out=out_tile, in_=result[:])
 
-        start_batch_norm()
-        for g in range(SOURCE_PASSES):
-            regroup_values(0, g, shared=True)
-        keep_warm(4)
+        load_function_table()
+        fold_batch_norm()
+        keep_warm(7)
+        regroup_values(0, 0, shared=True)
+        quantise_values(0, 0)
         flip_affinity(0, 0)
-        keep_warm(4)
-        for g in range(SOURCE_PASSES):
-            quantise_values(0, g)
-        quantise_affinity(0, 0)
+        keep_warm(3)
+        regroup_values(0, 1, shared=True)
         flip_affinity(0, 1)
-        keep_warm(2)
+        keep_warm(1)
+        quantise_affinity(0, 0)
+        quantise_values(0, 1)
         for c in range(STEPS):
-            if c + AHEAD < STEPS:
-                flip_affinity(*divmod(c + AHEAD, CHUNKS))
-            if c == 0:
-                keep_warm(2)
-            aggregate(*divmod(c, CHUNKS))
-            if c == 1:
-                batch_norm_std()
-            if c + 1 < STEPS:
-                quantise_affinity(*divmod(c + 1, CHUNKS))
-            if c == 2:
-                finish_batch_norm()
-            if c % 2 == 0 and c > 0:
-                quantise_y(*divmod(c // 2 - 1, HALVES))
-            if c == STEPS - 1:
-                quantise_y(BATCH - 1, HALVES - 1)
-            if CHUNKS - 1 <= c < STEPS - 1:
-                shift_residual(0, 2 * (c - CHUNKS + 1), "V")
-                shift_residual(0, 2 * (c - CHUNKS + 1) + 1, "S")
             if c in (1, 2):
+                aggregate(0, c, [0])
                 flip_weights(2 * (c - 1))
                 flip_weights(2 * (c - 1) + 1)
-            if c == 2:
+                aggregate(0, c, [1])
+            else:
+                aggregate(*divmod(c, CHUNKS))
+            if c > 0 and c % 2 == 0:
+                quantise_y(*divmod(c // 2 - 1, HALVES))
+            if c + AHEAD < STEPS:
+                flip_affinity(*divmod(c + AHEAD, CHUNKS))
+            if c + 1 < STEPS:
+                quantise_affinity(*divmod(c + 1, CHUNKS))
+            if c == 1:
                 for g in range(SOURCE_PASSES):
                     regroup_values(1, g)
+            elif c == 2:
                 for g in range(SOURCE_PASSES):
                     quantise_values(1, g)
-            if c == 3:
+            elif c == 3:
                 quantise_weights()
+                for r in (0, 2):
+                    shift_residual(0, r, "V")
+            elif c == 4:
+                for r in (1, 3):
+                    shift_residual(0, r, "S")
+                for r in (4, 6):
+                    shift_residual(0, r, "V")
+            elif c == 6:
+                for r in (5, 7):
+                    shift_residual(0, r, "S")
             if c >= CHUNKS:
                 project(0, 2 * (c - CHUNKS))
+                if c == STEPS - 1:
+                    quantise_y(BATCH - 1, HALVES - 1)
                 project(0, 2 * (c - CHUNKS) + 1)
         for r in range(CHANNEL_TILES):
             shift_residual(1, r, "S")

@@ -89,16 +89,16 @@ def tile_sgcam_pb_kernel(
         aff[0, 1] = load_affinity(0, 1)
         aff[0, 2] = load_affinity(0, 2)
         aff[0, 3] = load_affinity(0, 3)
-        w_rows[0] = load_weights(0)
-        w_rows[1] = load_weights(1)
-        gx_raw[1, 0] = load_values(1, 0)
-        gx_raw[1, 1] = load_values(1, 1)
-        aff[1, 0] = load_affinity(1, 0)
         var_bf = load_vector(bn_var, "var_bf")
         gamma_bf = load_vector(bn_gamma, "gamma_bf")
         bias_bf = load_vector(w_b, "bias_bf")
         mean_bf = load_vector(bn_mean, "mean_bf")
         beta_bf = load_vector(bn_beta, "beta_bf")
+        w_rows[0] = load_weights(0)
+        w_rows[1] = load_weights(1)
+        gx_raw[1, 0] = load_values(1, 0)
+        gx_raw[1, 1] = load_values(1, 1)
+        aff[1, 0] = load_affinity(1, 0)
         aff[1, 1] = load_affinity(1, 1)
         x_rows[0, 0] = load_residual(0, 0)
         aff[1, 2] = load_affinity(1, 2)
@@ -230,16 +230,18 @@ def tile_sgcam_pb_kernel(
         shift = const.tile([P, CHANNEL_TILES], F32)
 
         def load_function_table():
-            nc.scalar.activation(out=shift[:, :1], in_=dummy[:, :1], func=ACT.Identity)
+            nc.scalar.activation(out=shift[:, :1], in_=dummy[:, :1], func=ACT.Sqrt)
 
-        def fold_batch_norm():
+        def batch_norm_std():
             nc.gpsimd.tensor_scalar(
                 out=std[:], in0=var_bf[:], scalar1=1.0, scalar2=EPS, op0=ALU.mult, op1=ALU.add
             )
-            nc.gpsimd.memset(gain[:], -0.5)
-            nc.gpsimd.tensor_tensor(out=std[:], in0=std[:], in1=gain[:], op=ALU.pow)
-            nc.gpsimd.tensor_mul(out=gain[:], in0=std[:], in1=gamma_bf[:])
             nc.gpsimd.tensor_sub(out=shift[:], in0=bias_bf[:], in1=mean_bf[:])
+            nc.scalar.activation(out=std[:], in_=std[:], func=ACT.Sqrt)
+
+        def fold_batch_norm():
+            nc.vector.reciprocal(out=gain[:], in_=std[:])
+            nc.gpsimd.tensor_mul(out=gain[:], in0=gain[:], in1=gamma_bf[:])
             nc.gpsimd.tensor_mul(out=shift[:], in0=shift[:], in1=gain[:])
             nc.gpsimd.tensor_add(out=shift[:], in0=shift[:], in1=beta_bf[:])
 
@@ -289,7 +291,6 @@ def tile_sgcam_pb_kernel(
                     nc.sync.dma_start(out=out_tile, in_=result[:])
 
         load_function_table()
-        fold_batch_norm()
         keep_warm(7)
         regroup_values(0, 0, shared=True)
         quantise_values(0, 0)
@@ -308,6 +309,8 @@ def tile_sgcam_pb_kernel(
                 aggregate(0, c, [1])
             else:
                 aggregate(*divmod(c, CHUNKS))
+            if c == 0:
+                batch_norm_std()
             if c > 0 and c % 2 == 0:
                 quantise_y(*divmod(c // 2 - 1, HALVES))
             if c + AHEAD < STEPS:
@@ -315,6 +318,7 @@ def tile_sgcam_pb_kernel(
             if c + 1 < STEPS:
                 quantise_affinity(*divmod(c + 1, CHUNKS))
             if c == 1:
+                fold_batch_norm()
                 for g in range(SOURCE_PASSES):
                     regroup_values(1, g)
             elif c == 2:

@@ -43,7 +43,8 @@ def tile_sgcam_pb_kernel(
         loads = ctx.enter_context(tc.tile_pool(name="loads", bufs=1))
         keep = ctx.enter_context(tc.tile_pool(name="keep", bufs=1))
         stage = ctx.enter_context(tc.tile_pool(name="stage", bufs=2))
-        chunk_pool = ctx.enter_context(tc.tile_pool(name="chunk", bufs=4))
+        chunk_pool = ctx.enter_context(tc.tile_pool(name="chunk", bufs=3))
+        result_pool = ctx.enter_context(tc.tile_pool(name="results", bufs=12))
         banks = ctx.enter_context(tc.psum_pool(name="banks", bufs=8))
         ctx.enter_context(tc.manual_schedule())
 
@@ -124,13 +125,13 @@ def tile_sgcam_pb_kernel(
 
         def regroup_values(b, g, shared=False):
             grouped = stage.tile([P, INNER, PACK], BF16, name="gx_grouped", align_bytes=64)
-            split = P if not shared else 3 * P // 4
-            for regroup, lo, hi in ((nc.vector.tensor_copy, 0, split), (nc.scalar.copy, split, P)):
-                if lo < hi:
-                    regroup(
-                        out=grouped[:].rearrange("q (t m) j -> q t m j", t=INNER_TILES)[:, :, lo:hi],
-                        in_=gx_raw[b, g][:].rearrange("q j (m t) -> q t m j", t=INNER_TILES)[:, :, lo:hi],
-                    )
+            for t in range(PACK):
+                regroup = nc.scalar.copy if shared and t == PACK - 1 else nc.vector.tensor_copy
+                u, e = divmod(t, 2)
+                regroup(
+                    out=grouped[:].rearrange("q (t a i) j -> q t a j i", t=INNER_TILES, i=8)[:, t],
+                    in_=gx_raw[b, g][:].rearrange("q j (a u i e) -> q u e a j i", u=2, i=8, e=2)[:, u, e],
+                )
             gx_grouped[b, g] = grouped
 
         def quantise_values(b, g):
@@ -207,13 +208,22 @@ def tile_sgcam_pb_kernel(
         w_codes = keep.tile([P, CHANNELS], U32, align_bytes=64)
         w_scales = keep.tile([P, CHANNELS], U8, align_bytes=64)
 
+        w_words = {}
+
+        def order_weights(h, copy=nc.vector.tensor_copy):
+            ordered = keep.tile([P, 2 * PACK * P], F32, name="w_words%d" % h)
+            copy(
+                out=ordered[:].rearrange("p (r u a i) -> p r u a i", r=PACK, u=2, i=8),
+                in_=w_rows[h][:].rearrange("p r k -> p (r k)").bitcast(F32).rearrange("p (r a u i) -> p r u a i", r=PACK, u=2, i=8),
+            )
+            w_words[h] = ordered
+
         def flip_weights(pair, copy_out=nc.scalar.copy):
-            words = w_rows[pair // 2][:].rearrange("p r k -> p (r k)").bitcast(F32)
             flipped = banks.tile([P, 2, 2, P], F32, name="w_flipped", tag="bank")
             for k in range(2):
                 for u in range(2):
-                    first = (2 * (pair % 2) + k) * (INNER // 2) + u
-                    nc.tensor.transpose(flipped[:, k, u, :], words[:, first : first + 2 * P - 1 : 2], ident_f32[:])
+                    first = ((2 * (pair % 2) + k) * 2 + u) * P
+                    nc.tensor.transpose(flipped[:, k, u, :], w_words[pair // 2][:, first : first + P], ident_f32[:])
             grouped_words = w_grouped[:].rearrange("q r p t -> q (r p t)").bitcast(F32)
             copy_out(
                 out=grouped_words[:, 2 * pair * 2 * P : (2 * pair + 2) * 2 * P].rearrange("q (k p u) -> q k p u", k=2, u=2),
@@ -248,7 +258,7 @@ def tile_sgcam_pb_kernel(
         results = {}
 
         def shift_residual(b, r, engine):
-            result = keep.tile([P, POINTS], F32, name="result%d%d" % (b, r))
+            result = result_pool.tile([P, POINTS], F32, name="result")
             x_tile = x_rows[b, r // (CHANNEL_TILES // 2)][:, r % (CHANNEL_TILES // 2), :]
             if engine == 'G':
                 nc.gpsimd.tensor_scalar(
@@ -317,6 +327,8 @@ def tile_sgcam_pb_kernel(
                 flip_affinity(*divmod(c + AHEAD, CHUNKS))
             if c + 1 < STEPS:
                 quantise_affinity(*divmod(c + 1, CHUNKS))
+            if c < 2:
+                order_weights(c)
             if c == 1:
                 fold_batch_norm()
                 for g in range(SOURCE_PASSES):

@@ -75,9 +75,15 @@ def tile_sgcam_pb_kernel(
             nc.sync.dma_start(out=rows[:], in_=w_w.rearrange("(p r) k -> p r k", r=CHANNEL_TILES)[:, half_rows, :])
             return rows
 
+        def load_whole_residual(b):
+            rows = loads.tile([P, CHANNEL_TILES, POINTS], BF16, name="x%d" % b)
+            nc.sync.dma_start(out=rows[:], in_=x[b].rearrange("(p r) n -> p r n", r=CHANNEL_TILES))
+            for h in range(2):
+                x_rows[b, h] = rows[:, h * CHANNEL_TILES // 2 : (h + 1) * CHANNEL_TILES // 2, :]
+
         def load_vector(vec, name):
             rows = const.tile([P, CHANNEL_TILES], BF16, name=name)
-            nc.sync.dma_start(out=rows[:], in_=vec.rearrange("(p r) -> p r", r=CHANNEL_TILES))
+            nc.gpsimd.dma_start(out=rows[:], in_=vec.rearrange("(p r) -> p r", r=CHANNEL_TILES))
             return rows
 
         gx_raw = {}
@@ -90,11 +96,6 @@ def tile_sgcam_pb_kernel(
         aff[0, 1] = load_affinity(0, 1)
         aff[0, 2] = load_affinity(0, 2)
         aff[0, 3] = load_affinity(0, 3)
-        var_bf = load_vector(bn_var, "var_bf")
-        gamma_bf = load_vector(bn_gamma, "gamma_bf")
-        bias_bf = load_vector(w_b, "bias_bf")
-        mean_bf = load_vector(bn_mean, "mean_bf")
-        beta_bf = load_vector(bn_beta, "beta_bf")
         w_rows[0] = load_weights(0)
         w_rows[1] = load_weights(1)
         gx_raw[1, 0] = load_values(1, 0)
@@ -103,13 +104,18 @@ def tile_sgcam_pb_kernel(
         aff[1, 1] = load_affinity(1, 1)
         x_rows[0, 0] = load_residual(0, 0)
         aff[1, 2] = load_affinity(1, 2)
-        aff[1, 3] = load_affinity(1, 3)
         x_rows[0, 1] = load_residual(0, 1)
-        x_rows[1, 0] = load_residual(1, 0)
-        x_rows[1, 1] = load_residual(1, 1)
+        aff[1, 3] = load_affinity(1, 3)
+        load_whole_residual(1)
 
         ident_f32 = const.tile([P, P], F32)
         masks.make_identity(nc, ident_f32[:])
+
+        var_bf = load_vector(bn_var, "var_bf")
+        gamma_bf = load_vector(bn_gamma, "gamma_bf")
+        bias_bf = load_vector(w_b, "bias_bf")
+        mean_bf = load_vector(bn_mean, "mean_bf")
+        beta_bf = load_vector(bn_beta, "beta_bf")
 
         dummy = const.tile([P, HALF], BF16)
         nc.vector.memset(dummy[:], 0.0)
@@ -338,16 +344,13 @@ def tile_sgcam_pb_kernel(
                     quantise_values(1, g)
             elif c == 3:
                 quantise_weights()
-                for r in (0, 2):
-                    shift_residual(0, r, "V")
-            elif c == 4:
-                for r in (1, 3):
-                    shift_residual(0, r, "S")
-                for r in (4, 6):
-                    shift_residual(0, r, "V")
-            elif c == 6:
-                for r in (5, 7):
-                    shift_residual(0, r, "S")
+            if c in (3, 5):
+                first = 2 * (c - 3)
+                shift_residual(0, first, "V")
+                shift_residual(0, first + 2, "V")
+                shift_residual(0, first + 1, "S")
+            elif c in (4, 6):
+                shift_residual(0, 2 * (c - 4) + 3, "S")
             if c >= CHUNKS:
                 project(0, 2 * (c - CHUNKS))
                 if c == STEPS - 1:

@@ -14,6 +14,7 @@ ACT = mybir.ActivationFunctionType
 P = 128
 PACK = 4
 K_PASS = P * PACK
+EIGHT = 8
 
 BATCH = 2
 POINTS = 1024
@@ -30,6 +31,7 @@ HALF = 512
 HALVES = POINTS // HALF
 STEPS = BATCH * CHUNKS
 AHEAD = 2
+DUMMY_N = 512
 
 FLOPS = 2 * BATCH * POINTS * POINTS * INNER + 2 * BATCH * CHANNELS * INNER * POINTS
 
@@ -49,11 +51,11 @@ def tile_sgcam_pb_kernel(
         ctx.enter_context(tc.manual_schedule())
 
         def load_values(b, g):
-            raw = loads.tile([P, PACK, INNER], BF16, name="gx_raw%d%d" % (b, g))
+            rows = loads.tile([P, PACK, INNER], BF16, name="gx%d%d" % (b, g))
             nc.sync.dma_start(
-                out=raw[:], in_=g_x[b, g * K_PASS : (g + 1) * K_PASS, :].rearrange("(q j) c -> q j c", j=PACK)
+                out=rows[:], in_=g_x[b, g * K_PASS : (g + 1) * K_PASS, :].rearrange("(q t) c -> q t c", t=PACK)
             )
-            return raw
+            return rows
 
         def load_affinity(b, i):
             rows = loads.tile([P, 2, POINTS], BF16, name="aff%d%d" % (b, i))
@@ -63,53 +65,47 @@ def tile_sgcam_pb_kernel(
             )
             return rows
 
-        def load_residual(b, h):
-            rows = loads.tile([P, CHANNEL_TILES // 2, POINTS], BF16, name="x%d%d" % (b, h))
-            half_rows = slice(h * CHANNEL_TILES // 2, (h + 1) * CHANNEL_TILES // 2)
-            nc.sync.dma_start(out=rows[:], in_=x[b].rearrange("(p r) n -> p r n", r=CHANNEL_TILES)[:, half_rows, :])
-            return rows
-
         def load_weights(h):
             rows = loads.tile([P, CHANNEL_TILES // 2, INNER], BF16, name="w%d" % h)
-            half_rows = slice(h * CHANNEL_TILES // 2, (h + 1) * CHANNEL_TILES // 2)
-            nc.sync.dma_start(out=rows[:], in_=w_w.rearrange("(p r) k -> p r k", r=CHANNEL_TILES)[:, half_rows, :])
+            half = slice(h * CHANNEL_TILES // 2, (h + 1) * CHANNEL_TILES // 2)
+            nc.sync.dma_start(out=rows[:], in_=w_w.rearrange("(p r) k -> p r k", r=CHANNEL_TILES)[:, half, :])
             return rows
 
-        def load_whole_residual(b):
-            rows = loads.tile([P, CHANNEL_TILES, POINTS], BF16, name="x%d" % b)
-            nc.sync.dma_start(out=rows[:], in_=x[b].rearrange("(p r) n -> p r n", r=CHANNEL_TILES))
-            for h in range(2):
-                x_rows[b, h] = rows[:, h * CHANNEL_TILES // 2 : (h + 1) * CHANNEL_TILES // 2, :]
+        def load_residual(b, first, count):
+            rows = loads.tile([P, count, POINTS], BF16, name="x%d%d" % (b, first))
+            nc.sync.dma_start(
+                out=rows[:], in_=x[b].rearrange("(p r) n -> p r n", r=CHANNEL_TILES)[:, first : first + count, :]
+            )
+            for k in range(count):
+                x_tiles[b, first + k] = rows[:, k, :]
 
         def load_vector(vec, name):
             rows = const.tile([P, CHANNEL_TILES], BF16, name=name)
             nc.gpsimd.dma_start(out=rows[:], in_=vec.rearrange("(p r) -> p r", r=CHANNEL_TILES))
             return rows
 
-        gx_raw = {}
-        aff = {}
+        gx_rows = {}
+        aff_rows = {}
         w_rows = {}
-        x_rows = {}
-        gx_raw[0, 0] = load_values(0, 0)
-        aff[0, 0] = load_affinity(0, 0)
-        gx_raw[0, 1] = load_values(0, 1)
-        aff[0, 1] = load_affinity(0, 1)
-        aff[0, 2] = load_affinity(0, 2)
-        aff[0, 3] = load_affinity(0, 3)
-        w_rows[0] = load_weights(0)
-        w_rows[1] = load_weights(1)
-        gx_raw[1, 0] = load_values(1, 0)
-        gx_raw[1, 1] = load_values(1, 1)
-        aff[1, 0] = load_affinity(1, 0)
-        aff[1, 1] = load_affinity(1, 1)
-        x_rows[0, 0] = load_residual(0, 0)
-        aff[1, 2] = load_affinity(1, 2)
-        x_rows[0, 1] = load_residual(0, 1)
-        aff[1, 3] = load_affinity(1, 3)
-        load_whole_residual(1)
+        x_tiles = {}
+        for g in range(SOURCE_PASSES):
+            gx_rows[0, g] = load_values(0, g)
+            if g == 0:
+                aff_rows[0, 0] = load_affinity(0, 0)
+        for i in range(1, CHUNKS):
+            aff_rows[0, i] = load_affinity(0, i)
+        for h in range(2):
+            w_rows[h] = load_weights(h)
+        for g in range(SOURCE_PASSES):
+            gx_rows[1, g] = load_values(1, g)
+        for i in range(CHUNKS):
+            if i >= CHUNKS // 2:
+                load_residual(0, (i - CHUNKS // 2) * CHANNEL_TILES // 2, CHANNEL_TILES // 2)
+            aff_rows[1, i] = load_affinity(1, i)
+        load_residual(1, 0, CHANNEL_TILES)
 
-        ident_f32 = const.tile([P, P], F32)
-        masks.make_identity(nc, ident_f32[:])
+        ident = const.tile([P, P], F32)
+        masks.make_identity(nc, ident[:])
 
         var_bf = load_vector(bn_var, "var_bf")
         gamma_bf = load_vector(bn_gamma, "gamma_bf")
@@ -117,11 +113,11 @@ def tile_sgcam_pb_kernel(
         mean_bf = load_vector(bn_mean, "mean_bf")
         beta_bf = load_vector(bn_beta, "beta_bf")
 
-        dummy = const.tile([P, HALF], BF16)
+        dummy = const.tile([P, DUMMY_N], BF16)
         nc.vector.memset(dummy[:], 0.0)
 
         def keep_warm(count):
-            bank = banks.tile([P, HALF], F32, name="warm_bank", tag="bank")
+            bank = banks.tile([P, DUMMY_N], F32, name="dummy_bank", tag="bank")
             for k in range(count):
                 nc.tensor.matmul(out=bank[:], lhsT=dummy[:, :P], rhs=dummy[:], start=True, stop=True)
 
@@ -129,14 +125,14 @@ def tile_sgcam_pb_kernel(
         gx_codes = {}
         gx_scales = {}
 
-        def regroup_values(b, g, shared=False):
+        def regroup_values(b, g, scalar_tiles=0):
             grouped = stage.tile([P, INNER, PACK], BF16, name="gx_grouped", align_bytes=64)
-            for t in range(PACK):
-                regroup = nc.scalar.copy if shared and t == PACK - 1 else nc.vector.tensor_copy
+            for t in range(INNER_TILES):
                 u, e = divmod(t, 2)
+                regroup = nc.vector.tensor_copy if t < INNER_TILES - scalar_tiles else nc.scalar.copy
                 regroup(
-                    out=grouped[:].rearrange("q (t a i) j -> q t a j i", t=INNER_TILES, i=8)[:, t],
-                    in_=gx_raw[b, g][:].rearrange("q j (a u i e) -> q u e a j i", u=2, i=8, e=2)[:, u, e],
+                    out=grouped[:].rearrange("q (t a i) j -> q t a j i", t=INNER_TILES, i=EIGHT)[:, t],
+                    in_=gx_rows[b, g][:].rearrange("q j (a u i e) -> q u e a j i", u=2, i=EIGHT, e=2)[:, u, e],
                 )
             gx_grouped[b, g] = grouped
 
@@ -154,18 +150,18 @@ def tile_sgcam_pb_kernel(
         aff_scales = {}
 
         def flip_affinity(b, i):
-            words = aff[b, i][:].rearrange("p j m -> p (j m)").bitcast(F32)
+            words = aff_rows[b, i][:].rearrange("p j m -> p (j m)").bitcast(F32)
             grouped = chunk_pool.tile([P, SOURCE_PASSES * CHUNK * PACK], BF16, name="aff_grouped", align_bytes=64)
             grouped_words = grouped[:].bitcast(F32).rearrange(
-                "q (g p j u) -> q g p j u", g=SOURCE_PASSES, j=2, u=2
+                "q (g p j v) -> q g p j v", g=SOURCE_PASSES, j=2, v=2
             )
             for g in range(SOURCE_PASSES):
                 flipped = banks.tile([P, 2, 2, P], F32, name="flipped", tag="bank")
                 for j in range(2):
-                    for u in range(2):
-                        first = j * (POINTS // 2) + g * (K_PASS // 2) + u
-                        nc.tensor.transpose(flipped[:, j, u, :], words[:, first : first + 2 * P - 1 : 2], ident_f32[:])
-                nc.scalar.copy(out=grouped_words[:, g], in_=flipped[:].rearrange("q j u p -> q p j u"))
+                    for v in range(2):
+                        first = j * (POINTS // 2) + g * (K_PASS // 2) + v
+                        nc.tensor.transpose(flipped[:, j, v, :], words[:, first : first + 2 * P - 1 : 2], ident[:])
+                nc.scalar.copy(out=grouped_words[:, g], in_=flipped[:].rearrange("q j v p -> q p j v"))
             aff_grouped[b, i] = grouped
 
         def quantise_affinity(b, i):
@@ -179,27 +175,26 @@ def tile_sgcam_pb_kernel(
         y_codes = {}
         y_scales = {}
 
-        def aggregate(b, i, blocks=range(CHUNK // P)):
+        def aggregate(b, i, s):
             h, k = divmod(i, HALF // CHUNK)
-            if k == 0 and 0 in blocks:
+            if k == 0 and s == 0:
                 y_grouped[b, h] = stage.tile([P, HALF, PACK], BF16, name="y_grouped", align_bytes=64)
-            for s in blocks:
-                y_bank = banks.tile([P, INNER_TILES, P], F32, name="y_bank", tag="bank")
-                for t in range(INNER_TILES):
-                    for g in range(SOURCE_PASSES):
-                        ci = slice(t * P, (t + 1) * P)
-                        pts = slice(g * CHUNK + s * P, g * CHUNK + (s + 1) * P)
-                        nc.tensor.matmul_mx(
-                            out=y_bank[:, t, :],
-                            lhsT=gx_codes[b, g][:, ci].bitcast(FP8X4),
-                            lhsT_scale=gx_scales[b, g][:, ci],
-                            rhs=aff_codes[b, i][:, pts].bitcast(FP8X4),
-                            rhs_scale=aff_scales[b, i][:, pts],
-                            start=(g == 0),
-                            stop=(g == SOURCE_PASSES - 1),
-                        )
-                lo = k * CHUNK + s * P
-                nc.scalar.copy(out=y_grouped[b, h][:, lo : lo + P, :], in_=y_bank[:].rearrange("q t n -> q n t"))
+            y_bank = banks.tile([P, INNER_TILES, P], F32, name="y_bank", tag="bank")
+            for t in range(INNER_TILES):
+                for g in range(SOURCE_PASSES):
+                    cols = slice(t * P, (t + 1) * P)
+                    pts = slice(g * CHUNK + s * P, g * CHUNK + (s + 1) * P)
+                    nc.tensor.matmul_mx(
+                        out=y_bank[:, t, :],
+                        lhsT=gx_codes[b, g][:, cols].bitcast(FP8X4),
+                        lhsT_scale=gx_scales[b, g][:, cols],
+                        rhs=aff_codes[b, i][:, pts].bitcast(FP8X4),
+                        rhs_scale=aff_scales[b, i][:, pts],
+                        start=(g == 0),
+                        stop=(g == SOURCE_PASSES - 1),
+                    )
+            lo = k * CHUNK + s * P
+            nc.scalar.copy(out=y_grouped[b, h][:, lo : lo + P, :], in_=y_bank[:].rearrange("q t n -> q n t"))
 
         def quantise_y(b, h):
             codes = keep.tile([P, HALF], U32, name="y_codes%d%d" % (b, h), align_bytes=64)
@@ -210,29 +205,31 @@ def tile_sgcam_pb_kernel(
             y_codes[b, h] = codes
             y_scales[b, h] = scales
 
+        w_words = {}
         w_grouped = keep.tile([P, CHANNEL_TILES, P, PACK], BF16, align_bytes=64)
         w_codes = keep.tile([P, CHANNELS], U32, align_bytes=64)
         w_scales = keep.tile([P, CHANNELS], U8, align_bytes=64)
 
-        w_words = {}
-
-        def order_weights(h, copy=nc.vector.tensor_copy):
-            ordered = keep.tile([P, 2 * PACK * P], F32, name="w_words%d" % h)
-            copy(
-                out=ordered[:].rearrange("p (r u a i) -> p r u a i", r=PACK, u=2, i=8),
-                in_=w_rows[h][:].rearrange("p r k -> p (r k)").bitcast(F32).rearrange("p (r a u i) -> p r u a i", r=PACK, u=2, i=8),
+        def order_weights(h):
+            ordered = keep.tile([P, CHANNEL_TILES // 2 * INNER // 2], F32, name="w_words%d" % h)
+            nc.vector.tensor_copy(
+                out=ordered[:].rearrange("p (r u a i) -> p r u a i", r=CHANNEL_TILES // 2, u=2, i=EIGHT),
+                in_=w_rows[h][:].rearrange("p r k -> p (r k)").bitcast(F32).rearrange(
+                    "p (r a u i) -> p r u a i", r=CHANNEL_TILES // 2, u=2, i=EIGHT
+                ),
             )
             w_words[h] = ordered
 
-        def flip_weights(pair, copy_out=nc.scalar.copy):
+        def flip_weights(h, pair):
             flipped = banks.tile([P, 2, 2, P], F32, name="w_flipped", tag="bank")
             for k in range(2):
                 for u in range(2):
-                    first = ((2 * (pair % 2) + k) * 2 + u) * P
-                    nc.tensor.transpose(flipped[:, k, u, :], w_words[pair // 2][:, first : first + P], ident_f32[:])
+                    first = ((2 * pair + k) * 2 + u) * P
+                    nc.tensor.transpose(flipped[:, k, u, :], w_words[h][:, first : first + P], ident[:])
+            r = h * CHANNEL_TILES // 2 + 2 * pair
             grouped_words = w_grouped[:].rearrange("q r p t -> q (r p t)").bitcast(F32)
-            copy_out(
-                out=grouped_words[:, 2 * pair * 2 * P : (2 * pair + 2) * 2 * P].rearrange("q (k p u) -> q k p u", k=2, u=2),
+            nc.scalar.copy(
+                out=grouped_words[:, r * 2 * P : (r + 2) * 2 * P].rearrange("q (k p u) -> q k p u", k=2, u=2),
                 in_=flipped[:].rearrange("q k u p -> q k p u"),
             )
 
@@ -248,14 +245,12 @@ def tile_sgcam_pb_kernel(
         def load_function_table():
             nc.scalar.activation(out=shift[:, :1], in_=dummy[:, :1], func=ACT.Sqrt)
 
-        def batch_norm_std():
-            nc.gpsimd.tensor_scalar(
-                out=std[:], in0=var_bf[:], scalar1=1.0, scalar2=EPS, op0=ALU.mult, op1=ALU.add
-            )
+        def start_batch_norm():
+            nc.gpsimd.tensor_scalar(out=std[:], in0=var_bf[:], scalar1=1.0, scalar2=EPS, op0=ALU.mult, op1=ALU.add)
             nc.gpsimd.tensor_sub(out=shift[:], in0=bias_bf[:], in1=mean_bf[:])
             nc.scalar.activation(out=std[:], in_=std[:], func=ACT.Sqrt)
 
-        def fold_batch_norm():
+        def finish_batch_norm():
             nc.vector.reciprocal(out=gain[:], in_=std[:])
             nc.gpsimd.tensor_mul(out=gain[:], in0=gain[:], in1=gamma_bf[:])
             nc.gpsimd.tensor_mul(out=shift[:], in0=shift[:], in1=gain[:])
@@ -263,30 +258,25 @@ def tile_sgcam_pb_kernel(
 
         results = {}
 
-        def shift_residual(b, r, engine):
+        def shift_residual(b, r, on_vector=False):
             result = result_pool.tile([P, POINTS], F32, name="result")
-            x_tile = x_rows[b, r // (CHANNEL_TILES // 2)][:, r % (CHANNEL_TILES // 2), :]
-            if engine == 'G':
-                nc.gpsimd.tensor_scalar(
-                    out=result[:], in0=x_tile, scalar1=1.0, scalar2=shift[:, r : r + 1], op0=ALU.mult, op1=ALU.add
-                )
-            elif engine == 'V':
-                nc.vector.tensor_scalar_add(out=result[:], in0=x_tile, scalar1=shift[:, r : r + 1])
+            if on_vector:
+                nc.vector.tensor_scalar_add(out=result[:], in0=x_tiles[b, r], scalar1=shift[:, r : r + 1])
             else:
-                nc.scalar.activation(out=result[:], in_=x_tile, func=ACT.Identity, bias=shift[:, r : r + 1])
+                nc.scalar.activation(out=result[:], in_=x_tiles[b, r], func=ACT.Identity, bias=shift[:, r : r + 1])
             results[b, r] = result
 
-        def project(b, r, halves=range(HALVES)):
-            chans = slice(r * P, (r + 1) * P)
+        def project(b, r):
+            cols = slice(r * P, (r + 1) * P)
             result = results[b, r]
             out_tile = out[b].rearrange("(p r) n -> p r n", r=CHANNEL_TILES)[:, r, :]
             last_tile = b == BATCH - 1 and r == CHANNEL_TILES - 1
-            for h in halves:
+            for h in range(HALVES):
                 acc = banks.tile([P, HALF], F32, name="acc", tag="bank")
                 nc.tensor.matmul_mx(
                     out=acc[:],
-                    lhsT=w_codes[:, chans].bitcast(FP8X4),
-                    lhsT_scale=w_scales[:, chans],
+                    lhsT=w_codes[:, cols].bitcast(FP8X4),
+                    lhsT_scale=w_scales[:, cols],
                     rhs=y_codes[b, h][:].bitcast(FP8X4),
                     rhs_scale=y_scales[b, h][:],
                     start=True,
@@ -303,30 +293,30 @@ def tile_sgcam_pb_kernel(
                 )
                 if last_tile:
                     nc.sync.dma_start(out=out_tile[:, pts], in_=result[:, pts])
-                elif h == HALVES - 1:
-                    nc.sync.dma_start(out=out_tile, in_=result[:])
+            if not last_tile:
+                nc.sync.dma_start(out=out_tile, in_=result[:])
 
         load_function_table()
         keep_warm(7)
-        regroup_values(0, 0, shared=True)
+        regroup_values(0, 0, scalar_tiles=1)
         quantise_values(0, 0)
         flip_affinity(0, 0)
         keep_warm(3)
-        regroup_values(0, 1, shared=True)
+        regroup_values(0, 1, scalar_tiles=1)
         flip_affinity(0, 1)
         keep_warm(1)
         quantise_affinity(0, 0)
         quantise_values(0, 1)
+
         for c in range(STEPS):
+            chunk = divmod(c, CHUNKS)
+            aggregate(*chunk, 0)
             if c in (1, 2):
-                aggregate(0, c, [0])
-                flip_weights(2 * (c - 1))
-                flip_weights(2 * (c - 1) + 1)
-                aggregate(0, c, [1])
-            else:
-                aggregate(*divmod(c, CHUNKS))
-            if c == 0:
-                batch_norm_std()
+                for pair in range(2):
+                    flip_weights(c - 1, pair)
+            aggregate(*chunk, 1)
+            if c == 1:
+                start_batch_norm()
             if c > 0 and c % 2 == 0:
                 quantise_y(*divmod(c // 2 - 1, HALVES))
             if c + AHEAD < STEPS:
@@ -336,26 +326,21 @@ def tile_sgcam_pb_kernel(
             if c < 2:
                 order_weights(c)
             if c == 1:
-                fold_batch_norm()
                 for g in range(SOURCE_PASSES):
                     regroup_values(1, g)
             elif c == 2:
+                finish_batch_norm()
                 for g in range(SOURCE_PASSES):
                     quantise_values(1, g)
             elif c == 3:
                 quantise_weights()
-            if c in (3, 5):
-                first = 2 * (c - 3)
-                shift_residual(0, first, "V")
-                shift_residual(0, first + 2, "V")
-                shift_residual(0, first + 1, "S")
-            elif c in (4, 6):
-                shift_residual(0, 2 * (c - 4) + 3, "S")
+            for r in {3: (0, 1, 2), 4: (3,), 5: (4, 5), 6: (6, 7)}.get(c, ()):
+                shift_residual(0, r, on_vector=r in (0, 2, 4))
             if c >= CHUNKS:
                 project(0, 2 * (c - CHUNKS))
                 if c == STEPS - 1:
                     quantise_y(BATCH - 1, HALVES - 1)
                 project(0, 2 * (c - CHUNKS) + 1)
         for r in range(CHANNEL_TILES):
-            shift_residual(1, r, "S")
+            shift_residual(1, r)
             project(1, r)

from contextlib import ExitStack

import concourse.masks as masks
import concourse.mybir as mybir

F32 = mybir.dt.float32
BF16 = mybir.dt.bfloat16
U32 = mybir.dt.uint32
U8 = mybir.dt.uint8
FP8X4 = mybir.dt.float8_e4m3fn_x4
ALU = mybir.AluOpType
ACT = mybir.ActivationFunctionType

P = 128
PACK = 4
K_PASS = P * PACK
EIGHT = 8

BATCH = 2
POINTS = 1024
INNER = 512
CHANNELS = 1024
EPS = 1e-5

SOURCE_PASSES = POINTS // K_PASS
INNER_TILES = INNER // P
CHANNEL_TILES = CHANNELS // P
CHUNK = 2 * P
CHUNKS = POINTS // CHUNK
HALF = 512
HALVES = POINTS // HALF
STEPS = BATCH * CHUNKS
AHEAD = 2
DUMMY_N = 512

FLOPS = 2 * BATCH * POINTS * POINTS * INNER + 2 * BATCH * CHANNELS * INNER * POINTS


def tile_sgcam_pb_kernel(
    tc, affinity, g_x, w_w, w_b, bn_gamma, bn_beta, bn_mean, bn_var, x, out
):
    nc = tc.nc
    with ExitStack() as ctx:
        const = ctx.enter_context(tc.tile_pool(name="const", bufs=1))
        loads = ctx.enter_context(tc.tile_pool(name="loads", bufs=1))
        keep = ctx.enter_context(tc.tile_pool(name="keep", bufs=1))
        stage = ctx.enter_context(tc.tile_pool(name="stage", bufs=2))
        chunk_pool = ctx.enter_context(tc.tile_pool(name="chunk", bufs=3))
        result_pool = ctx.enter_context(tc.tile_pool(name="results", bufs=12))
        banks = ctx.enter_context(tc.psum_pool(name="banks", bufs=8))
        ctx.enter_context(tc.manual_schedule())

        def load_values(b, g):
            rows = loads.tile([P, PACK, INNER], BF16, name="gx%d%d" % (b, g))
            nc.sync.dma_start(
                out=rows[:], in_=g_x[b, g * K_PASS : (g + 1) * K_PASS, :].rearrange("(q t) c -> q t c", t=PACK)
            )
            return rows

        def load_affinity(b, i):
            rows = loads.tile([P, 2, POINTS], BF16, name="aff%d%d" % (b, i))
            nc.sync.dma_start(
                out=rows[:],
                in_=affinity[b, i * CHUNK : (i + 1) * CHUNK, :].rearrange("(p j) m -> p j m", j=2),
            )
            return rows

        def load_weights(h):
            rows = loads.tile([P, CHANNEL_TILES // 2, INNER], BF16, name="w%d" % h)
            half = slice(h * CHANNEL_TILES // 2, (h + 1) * CHANNEL_TILES // 2)
            nc.sync.dma_start(out=rows[:], in_=w_w.rearrange("(p r) k -> p r k", r=CHANNEL_TILES)[:, half, :])
            return rows

        def load_residual(b, first, count):
            rows = loads.tile([P, count, POINTS], BF16, name="x%d%d" % (b, first))
            nc.sync.dma_start(
                out=rows[:], in_=x[b].rearrange("(p r) n -> p r n", r=CHANNEL_TILES)[:, first : first + count, :]
            )
            for k in range(count):
                x_tiles[b, first + k] = rows[:, k, :]

        def load_vector(vec, name):
            rows = const.tile([P, CHANNEL_TILES], BF16, name=name)
            nc.gpsimd.dma_start(out=rows[:], in_=vec.rearrange("(p r) -> p r", r=CHANNEL_TILES))
            return rows

        gx_rows = {}
        aff_rows = {}
        w_rows = {}
        x_tiles = {}
        for g in range(SOURCE_PASSES):
            gx_rows[0, g] = load_values(0, g)
            if g == 0:
                aff_rows[0, 0] = load_affinity(0, 0)
        for i in range(1, CHUNKS):
            aff_rows[0, i] = load_affinity(0, i)
        for h in range(2):
            w_rows[h] = load_weights(h)
        for g in range(SOURCE_PASSES):
            gx_rows[1, g] = load_values(1, g)
        for i in range(CHUNKS):
            if i >= CHUNKS // 2:
                load_residual(0, (i - CHUNKS // 2) * CHANNEL_TILES // 2, CHANNEL_TILES // 2)
            aff_rows[1, i] = load_affinity(1, i)
        load_residual(1, 0, CHANNEL_TILES)

        ident = const.tile([P, P], F32)
        masks.make_identity(nc, ident[:])

        var_bf = load_vector(bn_var, "var_bf")
        gamma_bf = load_vector(bn_gamma, "gamma_bf")
        bias_bf = load_vector(w_b, "bias_bf")
        mean_bf = load_vector(bn_mean, "mean_bf")
        beta_bf = load_vector(bn_beta, "beta_bf")

        dummy = const.tile([P, DUMMY_N], BF16)
        nc.vector.memset(dummy[:], 0.0)

        def keep_warm(count):
            bank = banks.tile([P, DUMMY_N], F32, name="dummy_bank", tag="bank")
            for k in range(count):
                nc.tensor.matmul(out=bank[:], lhsT=dummy[:, :P], rhs=dummy[:], start=True, stop=True)

        gx_grouped = {}
        gx_codes = {}
        gx_scales = {}

        def regroup_values(b, g, scalar_tiles=0):
            grouped = stage.tile([P, INNER, PACK], BF16, name="gx_grouped", align_bytes=64)
            for t in range(INNER_TILES):
                u, e = divmod(t, 2)
                regroup = nc.vector.tensor_copy if t < INNER_TILES - scalar_tiles else nc.scalar.copy
                regroup(
                    out=grouped[:].rearrange("q (t a i) j -> q t a j i", t=INNER_TILES, i=EIGHT)[:, t],
                    in_=gx_rows[b, g][:].rearrange("q j (a u i e) -> q u e a j i", u=2, i=EIGHT, e=2)[:, u, e],
                )
            gx_grouped[b, g] = grouped

        def quantise_values(b, g):
            codes = keep.tile([P, INNER], U32, name="gx_codes%d%d" % (b, g), align_bytes=64)
            scales = keep.tile([P, INNER], U8, name="gx_scales%d%d" % (b, g), align_bytes=64)
            nc.vector.quantize_mx(
                out=codes[:].bitcast(FP8X4), scales=scales[:], in_=gx_grouped[b, g][:].rearrange("q c t -> q (c t)")
            )
            gx_codes[b, g] = codes
            gx_scales[b, g] = scales

        aff_grouped = {}
        aff_codes = {}
        aff_scales = {}

        def flip_affinity(b, i):
            words = aff_rows[b, i][:].rearrange("p j m -> p (j m)").bitcast(F32)
            grouped = chunk_pool.tile([P, SOURCE_PASSES * CHUNK * PACK], BF16, name="aff_grouped", align_bytes=64)
            grouped_words = grouped[:].bitcast(F32).rearrange(
                "q (g p j v) -> q g p j v", g=SOURCE_PASSES, j=2, v=2
            )
            for g in range(SOURCE_PASSES):
                flipped = banks.tile([P, 2, 2, P], F32, name="flipped", tag="bank")
                for j in range(2):
                    for v in range(2):
                        first = j * (POINTS // 2) + g * (K_PASS // 2) + v
                        nc.tensor.transpose(flipped[:, j, v, :], words[:, first : first + 2 * P - 1 : 2], ident[:])
                nc.scalar.copy(out=grouped_words[:, g], in_=flipped[:].rearrange("q j v p -> q p j v"))
            aff_grouped[b, i] = grouped

        def quantise_affinity(b, i):
            codes = chunk_pool.tile([P, SOURCE_PASSES * CHUNK], U32, name="aff_codes", align_bytes=64)
            scales = chunk_pool.tile([P, SOURCE_PASSES * CHUNK], U8, name="aff_scales", align_bytes=64)
            nc.vector.quantize_mx(out=codes[:].bitcast(FP8X4), scales=scales[:], in_=aff_grouped[b, i][:])
            aff_codes[b, i] = codes
            aff_scales[b, i] = scales

        y_grouped = {}
        y_codes = {}
        y_scales = {}

        def aggregate(b, i, s):
            h, k = divmod(i, HALF // CHUNK)
            if k == 0 and s == 0:
                y_grouped[b, h] = stage.tile([P, HALF, PACK], BF16, name="y_grouped", align_bytes=64)
            y_bank = banks.tile([P, INNER_TILES, P], F32, name="y_bank", tag="bank")
            for t in range(INNER_TILES):
                for g in range(SOURCE_PASSES):
                    cols = slice(t * P, (t + 1) * P)
                    pts = slice(g * CHUNK + s * P, g * CHUNK + (s + 1) * P)
                    nc.tensor.matmul_mx(
                        out=y_bank[:, t, :],
                        lhsT=gx_codes[b, g][:, cols].bitcast(FP8X4),
                        lhsT_scale=gx_scales[b, g][:, cols],
                        rhs=aff_codes[b, i][:, pts].bitcast(FP8X4),
                        rhs_scale=aff_scales[b, i][:, pts],
                        start=(g == 0),
                        stop=(g == SOURCE_PASSES - 1),
                    )
            lo = k * CHUNK + s * P
            nc.scalar.copy(out=y_grouped[b, h][:, lo : lo + P, :], in_=y_bank[:].rearrange("q t n -> q n t"))

        def quantise_y(b, h):
            codes = keep.tile([P, HALF], U32, name="y_codes%d%d" % (b, h), align_bytes=64)
            scales = keep.tile([P, HALF], U8, name="y_scales%d%d" % (b, h), align_bytes=64)
            nc.vector.quantize_mx(
                out=codes[:].bitcast(FP8X4), scales=scales[:], in_=y_grouped[b, h][:].rearrange("q n t -> q (n t)")
            )
            y_codes[b, h] = codes
            y_scales[b, h] = scales

        w_words = {}
        w_grouped = keep.tile([P, CHANNEL_TILES, P, PACK], BF16, align_bytes=64)
        w_codes = keep.tile([P, CHANNELS], U32, align_bytes=64)
        w_scales = keep.tile([P, CHANNELS], U8, align_bytes=64)

        def order_weights(h):
            ordered = keep.tile([P, CHANNEL_TILES // 2 * INNER // 2], F32, name="w_words%d" % h)
            nc.vector.tensor_copy(
                out=ordered[:].rearrange("p (r u a i) -> p r u a i", r=CHANNEL_TILES // 2, u=2, i=EIGHT),
                in_=w_rows[h][:].rearrange("p r k -> p (r k)").bitcast(F32).rearrange(
                    "p (r a u i) -> p r u a i", r=CHANNEL_TILES // 2, u=2, i=EIGHT
                ),
            )
            w_words[h] = ordered

        def flip_weights(h, pair):
            flipped = banks.tile([P, 2, 2, P], F32, name="w_flipped", tag="bank")
            for k in range(2):
                for u in range(2):
                    first = ((2 * pair + k) * 2 + u) * P
                    nc.tensor.transpose(flipped[:, k, u, :], w_words[h][:, first : first + P], ident[:])
            r = h * CHANNEL_TILES // 2 + 2 * pair
            grouped_words = w_grouped[:].rearrange("q r p t -> q (r p t)").bitcast(F32)
            nc.scalar.copy(
                out=grouped_words[:, r * 2 * P : (r + 2) * 2 * P].rearrange("q (k p u) -> q k p u", k=2, u=2),
                in_=flipped[:].rearrange("q k u p -> q k p u"),
            )

        def quantise_weights():
            nc.vector.quantize_mx(
                out=w_codes[:].bitcast(FP8X4), scales=w_scales[:], in_=w_grouped[:].rearrange("q r p t -> q (r p t)")
            )

        std = const.tile([P, CHANNEL_TILES], F32)
        gain = const.tile([P, CHANNEL_TILES], F32)
        shift = const.tile([P, CHANNEL_TILES], F32)

        def load_function_table():
            nc.scalar.activation(out=shift[:, :1], in_=dummy[:, :1], func=ACT.Sqrt)

        def start_batch_norm():
            nc.gpsimd.tensor_scalar(out=std[:], in0=var_bf[:], scalar1=1.0, scalar2=EPS, op0=ALU.mult, op1=ALU.add)
            nc.gpsimd.tensor_sub(out=shift[:], in0=bias_bf[:], in1=mean_bf[:])
            nc.scalar.activation(out=std[:], in_=std[:], func=ACT.Sqrt)

        def finish_batch_norm():
            nc.vector.reciprocal(out=gain[:], in_=std[:])
            nc.gpsimd.tensor_mul(out=gain[:], in0=gain[:], in1=gamma_bf[:])
            nc.gpsimd.tensor_mul(out=shift[:], in0=shift[:], in1=gain[:])
            nc.gpsimd.tensor_add(out=shift[:], in0=shift[:], in1=beta_bf[:])

        results = {}

        def shift_residual(b, r, on_vector=False):
            result = result_pool.tile([P, POINTS], F32, name="result")
            if on_vector:
                nc.vector.tensor_scalar_add(out=result[:], in0=x_tiles[b, r], scalar1=shift[:, r : r + 1])
            else:
                nc.scalar.activation(out=result[:], in_=x_tiles[b, r], func=ACT.Identity, bias=shift[:, r : r + 1])
            results[b, r] = result

        def project(b, r):
            cols = slice(r * P, (r + 1) * P)
            result = results[b, r]
            out_tile = out[b].rearrange("(p r) n -> p r n", r=CHANNEL_TILES)[:, r, :]
            last_tile = b == BATCH - 1 and r == CHANNEL_TILES - 1
            for h in range(HALVES):
                acc = banks.tile([P, HALF], F32, name="acc", tag="bank")
                nc.tensor.matmul_mx(
                    out=acc[:],
                    lhsT=w_codes[:, cols].bitcast(FP8X4),
                    lhsT_scale=w_scales[:, cols],
                    rhs=y_codes[b, h][:].bitcast(FP8X4),
                    rhs_scale=y_scales[b, h][:],
                    start=True,
                    stop=True,
                )
                pts = slice(h * HALF, (h + 1) * HALF)
                nc.vector.scalar_tensor_tensor(
                    out=result[:, pts],
                    in0=acc[:],
                    scalar=gain[:, r : r + 1],
                    in1=result[:, pts],
                    op0=ALU.mult,
                    op1=ALU.add,
                )
                if last_tile:
                    nc.sync.dma_start(out=out_tile[:, pts], in_=result[:, pts])
            if not last_tile:
                nc.sync.dma_start(out=out_tile, in_=result[:])

        load_function_table()
        keep_warm(7)
        regroup_values(0, 0, scalar_tiles=1)
        quantise_values(0, 0)
        flip_affinity(0, 0)
        keep_warm(3)
        regroup_values(0, 1, scalar_tiles=1)
        flip_affinity(0, 1)
        keep_warm(1)
        quantise_affinity(0, 0)
        quantise_values(0, 1)

        for c in range(STEPS):
            chunk = divmod(c, CHUNKS)
            aggregate(*chunk, 0)
            if c in (1, 2):
                for pair in range(2):
                    flip_weights(c - 1, pair)
            aggregate(*chunk, 1)
            if c == 1:
                start_batch_norm()
            if c > 0 and c % 2 == 0:
                quantise_y(*divmod(c // 2 - 1, HALVES))
            if c + AHEAD < STEPS:
                flip_affinity(*divmod(c + AHEAD, CHUNKS))
            if c + 1 < STEPS:
                quantise_affinity(*divmod(c + 1, CHUNKS))
            if c < 2:
                order_weights(c)
            if c == 1:
                for g in range(SOURCE_PASSES):
                    regroup_values(1, g)
            elif c == 2:
                finish_batch_norm()
                for g in range(SOURCE_PASSES):
                    quantise_values(1, g)
            elif c == 3:
                quantise_weights()
            for r in {3: (0, 1, 2), 4: (3,), 5: (4, 5), 6: (6, 7)}.get(c, ()):
                shift_residual(0, r, on_vector=r in (0, 2, 4))
            if c >= CHUNKS:
                project(0, 2 * (c - CHUNKS))
                if c == STEPS - 1:
                    quantise_y(BATCH - 1, HALVES - 1)
                project(0, 2 * (c - CHUNKS) + 1)
        for r in range(CHANNEL_TILES):
            shift_residual(1, r)
            project(1, r)
